import numpy as np
import ml_dtypes


def mxq(x, axis, fmt="e4m3"):
    dtype, down = {"e4m3": (ml_dtypes.float8_e4m3fn, 7), "e5m2": (ml_dtypes.float8_e5m2, 14)}[fmt]
    v = np.moveaxis(np.asarray(x, np.float32).astype(ml_dtypes.bfloat16).astype(np.float64), axis, -1)
    blocks = v.reshape(v.shape[:-1] + (-1, 32))
    amax = np.abs(blocks).max(-1, keepdims=True)
    byte = np.maximum(np.where(amax > 0, np.frexp(amax)[1] - 1 + 127, 0) - down, 1)
    scale = np.exp2(byte - 127.0)
    codes = (blocks / scale).astype(np.float32).astype(dtype).astype(np.float64)
    return np.moveaxis((codes * scale).reshape(v.shape), -1, axis)


WIDE = False


def mx_kscale(k):
    if not WIDE:
        return np.ones(k)
    levels = np.array([10, -10, 5, -5, 0])
    if k % 512:
        return np.exp2(np.random.permutation(np.resize(levels, k // 32))).repeat(32)
    a = np.empty((k // 512, 16))
    for p in range(k // 512):
        a[p, :8] = np.random.permutation(np.resize(levels, 8))
        for g in range(8):
            far = levels[np.abs(levels - a[p, g]) >= 10]
            a[p, g + 8] = far[np.random.randint(len(far))]
    return np.exp2(a.ravel()).repeat(32)


BF16 = ml_dtypes.bfloat16


def bf(x):
    return np.asarray(x, np.float32).astype(BF16)


def f64(x):
    return np.asarray(x).astype(np.float64)


B, C, H, W = 4, 512, 32, 32
N = H * W
C3 = 3 * C
EPS = 1e-4


def weight_norm(v, g):
    return g[:, None] * v / np.sqrt((v * v).sum(axis=1, keepdims=True))


def setup_inputs():
    s = mx_kscale(C)
    lift = np.sqrt(np.mean(1.0 / (s * s)))
    amp = np.exp2(-2.0 - 7.0 * np.random.random((B, 1, H, W)))
    row = np.exp(0.5 * np.random.standard_normal((C3, 1)))
    return {"x": bf(np.random.standard_normal((B, C, H, W)) * amp * (s * lift)[None, :, None, None]),
            "v_qkv": bf(np.random.standard_normal((C3, C)) * row / np.sqrt(C) / s[None, :]),
            "g_qkv": bf(1.0 + 0.1 * np.random.standard_normal(C3))}


def reference(x, v_qkv, g_qkv):
    w = weight_norm(f64(v_qkv), f64(g_qkv))
    xt = f64(x).reshape(B, C, N)
    qkv = mxq(w, 1, "e4m3") @ mxq(xt, 1, "e4m3")
    rms = np.sqrt(np.mean(np.square(qkv), axis=1, keepdims=True)) + EPS
    return qkv / rms

@@ -1,0 +1,239 @@
+from contextlib import ExitStack
+import math
+
+import concourse.mybir as mybir
+from concourse.masks import make_identity
+
+F32 = mybir.dt.float32
+BF16 = mybir.dt.bfloat16
+U32 = mybir.dt.uint32
+U8 = mybir.dt.uint8
+FP8X4 = mybir.dt.float8_e4m3fn_x4
+ACT = mybir.ActivationFunctionType
+ALU = mybir.AluOpType
+AX = mybir.AxisListType
+
+B, C, N, O = 4, 512, 1024, 1536
+P = 128
+PACK = 4
+J = O // P
+HALF = 512
+EPS = 1e-4
+FLOPS = 2 * B * O * C * N
+
+LEAD = 6
+V_TILES = (1, 3, 5, 13, 21, 27)
+G_FROM = 19
+PIN = False
+
+
+def tile_admattentionblock_pa_t_kernel(tc, x, v_qkv, g_qkv, out):
+    nc = tc.nc
+    with ExitStack() as ctx:
+        if PIN:
+            ctx.enter_context(tc.manual_schedule())
+        keep = ctx.enter_context(tc.tile_pool(name="keep", bufs=1))
+        work = ctx.enter_context(tc.tile_pool(name="work", bufs=2))
+        stage = ctx.enter_context(tc.tile_pool(name="stage", bufs=8))
+        psum = ctx.enter_context(tc.psum_pool(name="psum", bufs=1))
+
+        g_sb = keep.tile([P, J], BF16)
+        nc.scalar.dma_start(out=g_sb[:], in_=g_qkv.rearrange("(p j) -> p j", j=J))
+        v_sb = keep.tile([P, J, C], BF16)
+        v_view = v_qkv.rearrange("(p j) c -> p j c", j=J)
+        for j0, j1 in ((0, 2), (2, 4), (4, 8), (8, 12)):
+            nc.sync.dma_start(out=v_sb[:, j0:j1, :], in_=v_view[:, j0:j1, :])
+        x_raw = []
+        for b in range(B):
+            xr = keep.tile([P, PACK, N], BF16, name="x_raw%d" % b)
+            nc.sync.dma_start(out=xr[:], in_=x[b].rearrange("(p t) h w -> p t (h w)", t=PACK))
+            x_raw.append(xr)
+
+        ident_bf = keep.tile([P, P], BF16)
+        make_identity(nc, ident_bf[:])
+        ident_f = keep.tile([P, P], F32)
+        make_identity(nc, ident_f[:])
+        one = keep.tile([P, 1], F32)
+        nc.vector.memset(one[:], 1.0)
+        warm = keep.tile([P, 1], F32)
+        nc.scalar.activation(out=warm[:], in_=one[:], func=ACT.Sqrt)
+
+        xc = [keep.tile([P, N], U32, align_bytes=64, name="xc%d" % b) for b in range(B)]
+        xs = [keep.tile([P, N], U8, align_bytes=64, name="xs%d" % b) for b in range(B)]
+        xgs = {}
+
+        def regroup_x(b, h):
+            xg = work.tile([P, HALF, PACK], BF16, align_bytes=64, tag="xg", bufs=1, name="xg")
+            src = x_raw[b][:, :, HALF * h:HALF * (h + 1)]
+            if b == 0:
+                nc.vector.tensor_copy(out=xg[:].rearrange("p (c i) t -> p c t i", i=4),
+                                      in_=src.rearrange("p t (c i) -> p c t i", i=4))
+            else:
+                nc.gpsimd.tensor_scalar(out=xg[:], in0=src.rearrange("p t n -> p n t"),
+                                        scalar1=1.0, scalar2=0.0, op0=ALU.mult, op1=ALU.add)
+            xgs[(b, h)] = xg
+
+        def quantise_x(b, h):
+            nc.vector.quantize_mx(
+                out=xc[b][:, HALF * h:HALF * (h + 1)].bitcast(FP8X4),
+                scales=xs[b][:, HALF * h:HALF * (h + 1)],
+                in_=xgs[(b, h)][:].rearrange("p n t -> p (n t)"))
+
+        ss = keep.tile([P, 3, 16], F32)
+        norm = keep.tile([P, J], F32)
+        rnorm = keep.tile([P, J], F32)
+        sc = keep.tile([P, J], F32)
+        w_bf = keep.tile([P, J, PACK, P], BF16)
+        wg = keep.tile([P, J, P, PACK], BF16, align_bytes=64)
+        wc = keep.tile([P, O], U32, align_bytes=64)
+        ws = keep.tile([P, O], U8, align_bytes=64)
+        for a in range(3):
+            for r in range(4):
+                j = 4 * a + r
+                if r < 2:
+                    junk_s = work.tile([P, C], BF16, tag="junk_s")
+                    nc.scalar.activation(out=junk_s[:], in_=v_sb[:, j, :], func=ACT.Square,
+                                         accum_out=ss[:, a, r:r + 1])
+                else:
+                    junk_v = work.tile([P, C], F32, tag="junk_v")
+                    nc.vector.scalar_tensor_tensor(out=junk_v[:], in0=v_sb[:, j, :], scalar=1.0,
+                                                   in1=v_sb[:, j, :], op0=ALU.mult, op1=ALU.mult,
+                                                   accum_out=ss[:, a, 6 + r:7 + r])
+            four = slice(4 * a, 4 * a + 4)
+            nc.scalar.activation(out=norm[:, four].rearrange("p (s e) -> p s e", e=2),
+                                 in_=ss[:, a, :].rearrange("p (s e) -> p s e", e=8)[:, :, 0:2],
+                                 func=ACT.Sqrt)
+            nc.vector.reciprocal(out=rnorm[:, four], in_=norm[:, four])
+            nc.vector.tensor_tensor(out=sc[:, four], in0=rnorm[:, four], in1=g_sb[:, four], op=ALU.mult)
+            for r in range(4):
+                j = 4 * a + r
+                nc.vector.tensor_scalar(out=w_bf[:, j], in0=v_sb[:, j, :].rearrange("p (c t) -> p t c", t=PACK),
+                                        scalar1=sc[:, j:j + 1], scalar2=None, op0=ALU.mult)
+                wt = psum.tile([P, PACK, P], BF16, tag="mm", bufs=4)
+                for t in range(PACK):
+                    nc.tensor.transpose(out=wt[:, t, :], in_=w_bf[:, j, t, :], identity=ident_bf[:])
+                nc.scalar.copy(out=wg[:, j], in_=wt[:].rearrange("p t o -> p o t"))
+            if a == 1:
+                regroup_x(0, 0)
+            nc.vector.quantize_mx(
+                out=wc[:, HALF * a:HALF * (a + 1)].bitcast(FP8X4),
+                scales=ws[:, HALF * a:HALF * (a + 1)],
+                in_=wg[:, 4 * a:4 * a + 4].rearrange("p j o t -> p (j o t)"))
+        quantise_x(0, 0)
+        regroup_x(0, 1)
+        quantise_x(0, 1)
+        regroup_x(1, 0)
+
+        inv_sqrt_o = 1.0 / math.sqrt(O)
+        rb = {}
+        accs = {}
+        mss = {}
+        sts = {}
+        rinvs = {}
+
+        def mx(ps, lw, lcols, rw, rcols):
+            nc.tensor.matmul_mx(out=ps[:], lhsT=lw[0][:, lcols].bitcast(FP8X4), lhsT_scale=lw[1][:, lcols],
+                                rhs=rw[0][:, rcols].bitcast(FP8X4), rhs_scale=rw[1][:, rcols],
+                                start=True, stop=True)
+
+        def square_bank(k, g):
+            b, i = divmod(k, 8)
+            u, ii = divmod(k, 4)
+            if u not in accs:
+                accs[u] = work.tile([P, 12], F32, tag="acc", name="acc")
+                mss[u] = work.tile([P, 4], F32, tag="ms", name="ms")
+            on_vector = k in V_TILES
+            if on_vector:
+                ps = psum.tile([P, HALF], F32, tag="mm", bufs=4, name="ps_sv")
+            else:
+                ps = psum.tile([P, HALF], F32, tag="sq", bufs=3, name="ps_sq")
+            mx(ps, (xc[b], xs[b]), slice(P * i, P * (i + 1)), (wc, ws), slice(HALF * g, HALF * (g + 1)))
+            if on_vector:
+                if g == 0:
+                    sts[k] = work.tile([P, 3, 6], F32, tag="st", name="st")
+                nc.vector.bn_stats(out=sts[k][:, g, :], in_=ps[:])
+                if g == 2:
+                    mv = work.tile([P, 2], F32, tag="mv")
+                    nc.vector.bn_aggr(out=mv[:], in_=sts[k][:].rearrange("p g s -> p (g s)"))
+                    nc.vector.scalar_tensor_tensor(out=mss[u][:, ii:ii + 1], in0=mv[:, 0:1],
+                                                   scalar=mv[:, 0:1], in1=mv[:, 1:2],
+                                                   op0=ALU.mult, op1=ALU.add)
+            else:
+                junk = work.tile([P, HALF], BF16, tag="junk")
+                nc.scalar.activation(out=junk[:], in_=ps[:], func=ACT.Square, scale=inv_sqrt_o,
+                                     accum_out=accs[u][:, 3 * ii + g:3 * ii + g + 1])
+                first = ii
+                while first > 0 and (k - (ii - first) - 1) not in V_TILES:
+                    first -= 1
+                if g == 2 and (ii == 3 or (k + 1) in V_TILES):
+                    nc.vector.tensor_reduce(
+                        out=mss[u][:, first:ii + 1],
+                        in_=accs[u][:, 3 * first:3 * ii + 3].rearrange("p (i g) -> p i g", g=3),
+                        axis=AX.X, op=ALU.add)
+
+        def chain_a(u):
+            rms = work.tile([P, 4], F32, tag="rms")
+            nc.scalar.activation(out=rms[:], in_=mss[u][:], func=ACT.Sqrt)
+            rme = work.tile([P, 4], F32, tag="rme")
+            nc.vector.tensor_scalar_add(out=rme[:], in0=rms[:], scalar1=EPS)
+            rinvs[u] = work.tile([P, 4], F32, tag="rinv", name="rinv")
+            nc.vector.reciprocal(out=rinvs[u][:], in_=rme[:])
+
+        def chain_b(u):
+            bc = psum.tile([P, HALF], F32, tag="bc", bufs=1)
+            for q in range(4):
+                nc.tensor.transpose(out=bc[:, P * q:P * (q + 1)],
+                                    in_=rinvs[u][:, q:q + 1].to_broadcast([P, P]),
+                                    identity=ident_f[:])
+            rb[u] = work.tile([P, HALF], F32, tag="rb", bufs=4, name="rb")
+            nc.scalar.copy(out=rb[u][:], in_=bc[:])
+
+        items = [(b, q, h) for b in range(B) for h in range(2) for q in range(4)]
+        ots = {}
+
+        def final_bank(m, jj):
+            b, q, h = items[m]
+            j = 3 * q + jj
+            cols = slice(HALF * h, HALF * (h + 1))
+            o_view = out[b].rearrange("(p j) n -> p j n", j=J)
+            if jj == 0:
+                ots[m] = stage.tile([P, 3, HALF], F32, tag="ot", name="ot")
+            dst = ots[m][:, jj, :]
+            ps = psum.tile([P, HALF], F32, tag="mm", bufs=4, name="ps_mm")
+            mx(ps, (wc, ws), slice(P * j, P * (j + 1)), (xc[b], xs[b]), cols)
+            if m >= G_FROM and jj == 0:
+                nc.scalar.copy(out=dst, in_=ps[:])
+                nc.gpsimd.tensor_tensor(out=dst, in0=dst, in1=rb[2 * b + h][:], op=ALU.mult)
+            else:
+                nc.vector.tensor_tensor(out=dst, in0=ps[:], in1=rb[2 * b + h][:], op=ALU.mult)
+            if m == len(items) - 1:
+                nc.sync.dma_start(out=o_view[:, j:j + 1, cols], in_=ots[m][:, jj:jj + 1, :])
+            elif jj == 2:
+                nc.sync.dma_start(out=o_view[:, 3 * q:3 * q + 3, cols], in_=ots[m][:])
+
+        n_tiles = 8 * B
+        for k in range(0, LEAD, 2):
+            for g in range(3):
+                square_bank(k, g)
+                square_bank(k + 1, g)
+                if k == 4 and g == 0:
+                    chain_b(0)
+            if k == 2:
+                chain_a(0)
+            if k == 4:
+                quantise_x(1, 0)
+                regroup_x(1, 1)
+        for r in range(LEAD, n_tiles + LEAD):
+            for g in range(3):
+                if r < n_tiles:
+                    square_bank(r, g)
+                final_bank(r - LEAD, g)
+            if r < n_tiles and r % 4 == 3:
+                chain_a(r // 4)
+            if r <= n_tiles and r % 4 == 0:
+                chain_b(r // 4 - 1)
+            if r % 4 == 1 and r // 4 < 2 * B - 1:
+                u = r // 4 + 1
+                quantise_x(u // 2, u % 2)
+                if u + 1 < 2 * B:
+                    regroup_x((u + 1) // 2, (u + 1) % 2)

@@ -18,45 +18,57 @@ P = 128
 PACK = 4
 J = O // P
 HALF = 512
+BANKS = O // HALF
 EPS = 1e-4
 FLOPS = 2 * B * O * C * N
 
-LEAD = 6
-V_TILES = (1, 3, 5, 13, 21, 27)
-G_FROM = 19
-PIN = False
+UNITS = [(0, 0, 256), (0, 256, 256), (0, 512, 512)] + [(b, h, HALF) for b in range(1, B) for h in (0, HALF)]
+V_TILES = (1, 7, 19)
+CHAIN_LAG = 2
 
 
 def tile_admattentionblock_pa_t_kernel(tc, x, v_qkv, g_qkv, out):
     nc = tc.nc
     with ExitStack() as ctx:
-        if PIN:
-            ctx.enter_context(tc.manual_schedule())
         keep = ctx.enter_context(tc.tile_pool(name="keep", bufs=1))
         work = ctx.enter_context(tc.tile_pool(name="work", bufs=2))
         stage = ctx.enter_context(tc.tile_pool(name="stage", bufs=8))
         psum = ctx.enter_context(tc.psum_pool(name="psum", bufs=1))
 
-        g_sb = keep.tile([P, J], BF16)
-        nc.scalar.dma_start(out=g_sb[:], in_=g_qkv.rearrange("(p j) -> p j", j=J))
+        g_bf = keep.tile([P, J], BF16)
+        nc.scalar.dma_start(out=g_bf[:], in_=g_qkv.rearrange("(p j) -> p j", j=J))
         v_sb = keep.tile([P, J, C], BF16)
         v_view = v_qkv.rearrange("(p j) c -> p j c", j=J)
-        for j0, j1 in ((0, 2), (2, 4), (4, 8), (8, 12)):
-            nc.sync.dma_start(out=v_sb[:, j0:j1, :], in_=v_view[:, j0:j1, :])
-        x_raw = []
-        for b in range(B):
-            xr = keep.tile([P, PACK, N], BF16, name="x_raw%d" % b)
-            nc.sync.dma_start(out=xr[:], in_=x[b].rearrange("(p t) h w -> p t (h w)", t=PACK))
-            x_raw.append(xr)
+        x_raw = {}
 
-        ident_bf = keep.tile([P, P], BF16)
-        make_identity(nc, ident_bf[:])
-        ident_f = keep.tile([P, P], F32)
-        make_identity(nc, ident_f[:])
+        def load_v(j0, j1):
+            nc.sync.dma_start(out=v_sb[:, j0:j1, :], in_=v_view[:, j0:j1, :])
+
+        def load_x(b, n0, n1):
+            view = x[b].rearrange("(p t) h w -> p t (h w)", t=PACK)
+            xr = keep.tile([P, PACK, n1 - n0], BF16, name="x_raw%d_%d" % (b, n0))
+            nc.sync.dma_start(out=xr[:], in_=view[:, :, n0:n1])
+            for n in range(n0, n1, HALF):
+                x_raw[b, n // HALF] = xr[:, :, n - n0:n - n0 + HALF]
+
+        with tc.manual_schedule():
+            for j in range(0, 6, 2):
+                load_v(j, j + 2)
+            load_x(0, 0, HALF)
+            load_v(6, 8)
+            load_v(8, 12)
+            load_x(0, HALF, N)
+            for b in range(1, B):
+                load_x(b, 0, N)
+
+        ident = keep.tile([P, P], F32)
+        make_identity(nc, ident[:])
         one = keep.tile([P, 1], F32)
         nc.vector.memset(one[:], 1.0)
         warm = keep.tile([P, 1], F32)
         nc.scalar.activation(out=warm[:], in_=one[:], func=ACT.Sqrt)
+        g_f = keep.tile([P, J], F32)
+        nc.gpsimd.tensor_copy(out=g_f[:], in_=g_bf[:])
 
         xc = [keep.tile([P, N], U32, align_bytes=64, name="xc%d" % b) for b in range(B)]
         xs = [keep.tile([P, N], U8, align_bytes=64, name="xs%d" % b) for b in range(B)]
@@ -64,7 +76,7 @@ def tile_admattentionblock_pa_t_kernel(tc, x, v_qkv, g_qkv, out):
 
         def regroup_x(b, h):
             xg = work.tile([P, HALF, PACK], BF16, align_bytes=64, tag="xg", bufs=1, name="xg")
-            src = x_raw[b][:, :, HALF * h:HALF * (h + 1)]
+            src = x_raw[b, h]
             if b == 0:
                 nc.vector.tensor_copy(out=xg[:].rearrange("p (c i) t -> p c t i", i=4),
                                       in_=src.rearrange("p t (c i) -> p c t i", i=4))
@@ -79,80 +91,123 @@ def tile_admattentionblock_pa_t_kernel(tc, x, v_qkv, g_qkv, out):
                 scales=xs[b][:, HALF * h:HALF * (h + 1)],
                 in_=xgs[(b, h)][:].rearrange("p n t -> p (n t)"))
 
-        ss = keep.tile([P, 3, 16], F32)
+        ss = keep.tile([P, J], F32)
         norm = keep.tile([P, J], F32)
         rnorm = keep.tile([P, J], F32)
-        sc = keep.tile([P, J], F32)
-        w_bf = keep.tile([P, J, PACK, P], BF16)
+        w_bf = keep.tile([P, J, C], BF16)
         wg = keep.tile([P, J, P, PACK], BF16, align_bytes=64)
         wc = keep.tile([P, O], U32, align_bytes=64)
         ws = keep.tile([P, O], U8, align_bytes=64)
-        for a in range(3):
-            for r in range(4):
-                j = 4 * a + r
-                if r < 2:
-                    junk_s = work.tile([P, C], BF16, tag="junk_s")
-                    nc.scalar.activation(out=junk_s[:], in_=v_sb[:, j, :], func=ACT.Square,
-                                         accum_out=ss[:, a, r:r + 1])
-                else:
-                    junk_v = work.tile([P, C], F32, tag="junk_v")
+
+        def norms(pair):
+            for j in (2 * pair, 2 * pair + 1):
+                if pair == 1:
+                    junk_v = work.tile([P, C], F32, tag="junk_v", name="junk_v")
                     nc.vector.scalar_tensor_tensor(out=junk_v[:], in0=v_sb[:, j, :], scalar=1.0,
                                                    in1=v_sb[:, j, :], op0=ALU.mult, op1=ALU.mult,
-                                                   accum_out=ss[:, a, 6 + r:7 + r])
-            four = slice(4 * a, 4 * a + 4)
-            nc.scalar.activation(out=norm[:, four].rearrange("p (s e) -> p s e", e=2),
-                                 in_=ss[:, a, :].rearrange("p (s e) -> p s e", e=8)[:, :, 0:2],
-                                 func=ACT.Sqrt)
-            nc.vector.reciprocal(out=rnorm[:, four], in_=norm[:, four])
-            nc.vector.tensor_tensor(out=sc[:, four], in0=rnorm[:, four], in1=g_sb[:, four], op=ALU.mult)
-            for r in range(4):
-                j = 4 * a + r
-                nc.vector.tensor_scalar(out=w_bf[:, j], in0=v_sb[:, j, :].rearrange("p (c t) -> p t c", t=PACK),
-                                        scalar1=sc[:, j:j + 1], scalar2=None, op0=ALU.mult)
-                wt = psum.tile([P, PACK, P], BF16, tag="mm", bufs=4)
-                for t in range(PACK):
-                    nc.tensor.transpose(out=wt[:, t, :], in_=w_bf[:, j, t, :], identity=ident_bf[:])
-                nc.scalar.copy(out=wg[:, j], in_=wt[:].rearrange("p t o -> p o t"))
-            if a == 1:
-                regroup_x(0, 0)
-            nc.vector.quantize_mx(
-                out=wc[:, HALF * a:HALF * (a + 1)].bitcast(FP8X4),
-                scales=ws[:, HALF * a:HALF * (a + 1)],
-                in_=wg[:, 4 * a:4 * a + 4].rearrange("p j o t -> p (j o t)"))
-        quantise_x(0, 0)
-        regroup_x(0, 1)
+                                                   accum_out=ss[:, j:j + 1])
+                else:
+                    junk_s = work.tile([P, C], BF16, tag="junk_s", name="junk_s")
+                    nc.scalar.activation(out=junk_s[:], in_=v_sb[:, j, :], func=ACT.Square,
+                                         accum_out=ss[:, j:j + 1])
+
+        def root(pair):
+            two = slice(2 * pair, 2 * pair + 2)
+            nc.scalar.activation(out=norm[:, two], in_=ss[:, two], func=ACT.Sqrt)
+
+        wts = {}
+
+        def scale_and_turn(pair):
+            two = slice(2 * pair, 2 * pair + 2)
+            nc.vector.reciprocal(out=rnorm[:, two], in_=norm[:, two])
+            wts[pair] = psum.tile([P, 2, 2, P], F32, tag="mm", bufs=4, name="wt")
+            for jj in range(2):
+                j = 2 * pair + jj
+                nc.vector.tensor_scalar(out=w_bf[:, j, :], in0=v_sb[:, j, :],
+                                        scalar1=rnorm[:, j:j + 1], scalar2=g_f[:, j:j + 1],
+                                        op0=ALU.mult, op1=ALU.mult)
+                words = w_bf[:, j, :].bitcast(F32)
+                for u in range(2):
+                    nc.tensor.transpose(out=wts[pair][:, jj, u, :], in_=words[:, u::2], identity=ident[:])
+
+        def gather_w(pair, copy):
+            dst = wg[:, 2 * pair:2 * pair + 2].rearrange("p j o t -> p (j o t)").bitcast(F32)
+            copy(out=dst.rearrange("p (j o u) -> p j o u", j=2, u=2),
+                 in_=wts[pair][:].rearrange("p j u o -> p j o u"))
+
+        def quantise_w(pair):
+            cols = slice(2 * P * pair, 2 * P * (pair + 1))
+            nc.vector.quantize_mx(out=wc[:, cols].bitcast(FP8X4), scales=ws[:, cols],
+                                  in_=wg[:, 2 * pair:2 * pair + 2].rearrange("p j o t -> p (j o t)"))
+
+        on_s, on_v = nc.scalar.copy, nc.vector.tensor_copy
+        with tc.manual_schedule():
+            norms(0)
+            root(0)
+            norms(1)
+            scale_and_turn(0)
+            norms(2)
+            root(1)
+            root(2)
+            scale_and_turn(1)
+            regroup_x(0, 0)
+            norms(3)
+            root(3)
+            scale_and_turn(2)
+            norms(4)
+            root(4)
+            scale_and_turn(3)
+            quantise_x(0, 0)
+            gather_w(0, on_s)
+            scale_and_turn(4)
+            norms(5)
+            root(5)
+            gather_w(1, on_v)
+            quantise_w(0)
+            scale_and_turn(5)
+            gather_w(2, on_s)
+            quantise_w(1)
+            gather_w(3, on_v)
+            gather_w(4, on_s)
+            quantise_w(2)
+            gather_w(5, on_s)
+            quantise_w(3)
+            quantise_w(4)
+            quantise_w(5)
+            regroup_x(0, 1)
         quantise_x(0, 1)
         regroup_x(1, 0)
 
         inv_sqrt_o = 1.0 / math.sqrt(O)
-        rb = {}
-        accs = {}
-        mss = {}
-        sts = {}
-        rinvs = {}
+        rb, accs, mss, sts, rinvs = {}, {}, {}, {}, {}
 
         def mx(ps, lw, lcols, rw, rcols):
-            nc.tensor.matmul_mx(out=ps[:], lhsT=lw[0][:, lcols].bitcast(FP8X4), lhsT_scale=lw[1][:, lcols],
+            nc.tensor.matmul_mx(out=ps, lhsT=lw[0][:, lcols].bitcast(FP8X4), lhsT_scale=lw[1][:, lcols],
                                 rhs=rw[0][:, rcols].bitcast(FP8X4), rhs_scale=rw[1][:, rcols],
                                 start=True, stop=True)
 
+        places = []
+        for u, (b, n0, width) in enumerate(UNITS):
+            for ii in range(width // P):
+                places.append((u, ii, width // P))
+
         def square_bank(k, g):
-            b, i = divmod(k, 8)
-            u, ii = divmod(k, 4)
+            b, i = divmod(k, N // P)
+            u, ii, count = places[k]
             if u not in accs:
-                accs[u] = work.tile([P, 12], F32, tag="acc", name="acc")
+                accs[u] = work.tile([P, 4 * BANKS], F32, tag="acc", name="acc")
                 mss[u] = work.tile([P, 4], F32, tag="ms", name="ms")
             on_vector = k in V_TILES
             if on_vector:
                 ps = psum.tile([P, HALF], F32, tag="mm", bufs=4, name="ps_sv")
             else:
                 ps = psum.tile([P, HALF], F32, tag="sq", bufs=3, name="ps_sq")
-            mx(ps, (xc[b], xs[b]), slice(P * i, P * (i + 1)), (wc, ws), slice(HALF * g, HALF * (g + 1)))
+            mx(ps[:], (xc[b], xs[b]), slice(P * i, P * (i + 1)), (wc, ws), slice(HALF * g, HALF * (g + 1)))
             if on_vector:
                 if g == 0:
-                    sts[k] = work.tile([P, 3, 6], F32, tag="st", name="st")
+                    sts[k] = work.tile([P, BANKS, 6], F32, tag="st", name="st")
                 nc.vector.bn_stats(out=sts[k][:, g, :], in_=ps[:])
-                if g == 2:
+                if g == BANKS - 1:
                     mv = work.tile([P, 2], F32, tag="mv")
                     nc.vector.bn_aggr(out=mv[:], in_=sts[k][:].rearrange("p g s -> p (g s)"))
                     nc.vector.scalar_tensor_tensor(out=mss[u][:, ii:ii + 1], in0=mv[:, 0:1],
@@ -161,79 +216,99 @@ def tile_admattentionblock_pa_t_kernel(tc, x, v_qkv, g_qkv, out):
             else:
                 junk = work.tile([P, HALF], BF16, tag="junk")
                 nc.scalar.activation(out=junk[:], in_=ps[:], func=ACT.Square, scale=inv_sqrt_o,
-                                     accum_out=accs[u][:, 3 * ii + g:3 * ii + g + 1])
-                first = ii
-                while first > 0 and (k - (ii - first) - 1) not in V_TILES:
-                    first -= 1
-                if g == 2 and (ii == 3 or (k + 1) in V_TILES):
+                                     accum_out=accs[u][:, BANKS * ii + g:BANKS * ii + g + 1])
+                if g == BANKS - 1 and (ii == count - 1 or (k + 1) in V_TILES):
                     nc.vector.tensor_reduce(
-                        out=mss[u][:, first:ii + 1],
-                        in_=accs[u][:, 3 * first:3 * ii + 3].rearrange("p (i g) -> p i g", g=3),
+                        out=mss[u][:, 0:ii + 1],
+                        in_=accs[u][:, 0:BANKS * (ii + 1)].rearrange("p (i g) -> p i g", g=BANKS),
                         axis=AX.X, op=ALU.add)
 
         def chain_a(u):
+            count = UNITS[u][2] // P
             rms = work.tile([P, 4], F32, tag="rms")
-            nc.scalar.activation(out=rms[:], in_=mss[u][:], func=ACT.Sqrt)
+            nc.scalar.activation(out=rms[:, 0:count], in_=mss[u][:, 0:count], func=ACT.Sqrt)
             rme = work.tile([P, 4], F32, tag="rme")
-            nc.vector.tensor_scalar_add(out=rme[:], in0=rms[:], scalar1=EPS)
+            nc.vector.tensor_scalar_add(out=rme[:, 0:count], in0=rms[:, 0:count], scalar1=EPS)
             rinvs[u] = work.tile([P, 4], F32, tag="rinv", name="rinv")
-            nc.vector.reciprocal(out=rinvs[u][:], in_=rme[:])
+            nc.vector.reciprocal(out=rinvs[u][:, 0:count], in_=rme[:, 0:count])
 
         def chain_b(u):
+            width = UNITS[u][2]
             bc = psum.tile([P, HALF], F32, tag="bc", bufs=1)
-            for q in range(4):
+            for q in range(width // P):
                 nc.tensor.transpose(out=bc[:, P * q:P * (q + 1)],
                                     in_=rinvs[u][:, q:q + 1].to_broadcast([P, P]),
-                                    identity=ident_f[:])
+                                    identity=ident[:])
             rb[u] = work.tile([P, HALF], F32, tag="rb", bufs=4, name="rb")
-            nc.scalar.copy(out=rb[u][:], in_=bc[:])
+            nc.scalar.copy(out=rb[u][:, 0:width], in_=bc[:, 0:width])
 
-        items = [(b, q, h) for b in range(B) for h in range(2) for q in range(4)]
+        finals = []
+        for u, (b, n0, width) in enumerate(UNITS):
+            per = HALF // width
+            group = 4 if width == 256 else 3
+            for j0 in range(0, J, group):
+                for jj in range(0, group, per):
+                    finals.append((u, j0, jj, per, group))
         ots = {}
 
-        def final_bank(m, jj):
-            b, q, h = items[m]
-            j = 3 * q + jj
-            cols = slice(HALF * h, HALF * (h + 1))
+        def final_bank(f, helped, alone):
+            u, j0, jj, per, group = finals[f]
+            b, n0, width = UNITS[u]
+            cols = slice(n0, n0 + width)
             o_view = out[b].rearrange("(p j) n -> p j n", j=J)
             if jj == 0:
-                ots[m] = stage.tile([P, 3, HALF], F32, tag="ot", name="ot")
-            dst = ots[m][:, jj, :]
+                ots[u, j0] = stage.tile([P, 3 * HALF], F32, tag="ot", name="ot")
+            ot = ots[u, j0][:, 0:group * width].rearrange("p (j n) -> p j n", j=group)
+            dst = ot[:, jj:jj + per, :]
             ps = psum.tile([P, HALF], F32, tag="mm", bufs=4, name="ps_mm")
-            mx(ps, (wc, ws), slice(P * j, P * (j + 1)), (xc[b], xs[b]), cols)
-            if m >= G_FROM and jj == 0:
-                nc.scalar.copy(out=dst, in_=ps[:])
-                nc.gpsimd.tensor_tensor(out=dst, in0=dst, in1=rb[2 * b + h][:], op=ALU.mult)
+            ps = ps[:].rearrange("p (j n) -> p j n", j=per)
+            for e in range(per):
+                j = j0 + jj + e
+                mx(ps[:, e, :], (wc, ws), slice(P * j, P * (j + 1)), (xc[b], xs[b]), cols)
+            r = rb[u][:, 0:width].unsqueeze(1).to_broadcast([P, per, width])
+            if helped:
+                nc.scalar.copy(out=dst, in_=ps)
+                nc.gpsimd.tensor_tensor(out=dst, in0=dst, in1=r, op=ALU.mult)
             else:
-                nc.vector.tensor_tensor(out=dst, in0=ps[:], in1=rb[2 * b + h][:], op=ALU.mult)
-            if m == len(items) - 1:
-                nc.sync.dma_start(out=o_view[:, j:j + 1, cols], in_=ots[m][:, jj:jj + 1, :])
-            elif jj == 2:
-                nc.sync.dma_start(out=o_view[:, 3 * q:3 * q + 3, cols], in_=ots[m][:])
+                nc.vector.tensor_tensor(out=dst, in0=ps, in1=r, op=ALU.mult)
+            if alone:
+                nc.sync.dma_start(out=o_view[:, j0 + jj:j0 + jj + per, cols], in_=dst)
+            elif jj + per == group:
+                nc.sync.dma_start(out=o_view[:, j0:j0 + group, cols], in_=ot)
 
-        n_tiles = 8 * B
-        for k in range(0, LEAD, 2):
-            for g in range(3):
-                square_bank(k, g)
-                square_bank(k + 1, g)
-                if k == 4 and g == 0:
-                    chain_b(0)
-            if k == 2:
-                chain_a(0)
-            if k == 4:
-                quantise_x(1, 0)
-                regroup_x(1, 1)
-        for r in range(LEAD, n_tiles + LEAD):
-            for g in range(3):
-                if r < n_tiles:
-                    square_bank(r, g)
-                final_bank(r - LEAD, g)
-            if r < n_tiles and r % 4 == 3:
-                chain_a(r // 4)
-            if r <= n_tiles and r % 4 == 0:
-                chain_b(r // 4 - 1)
-            if r % 4 == 1 and r // 4 < 2 * B - 1:
-                u = r // 4 + 1
-                quantise_x(u // 2, u % 2)
-                if u + 1 < 2 * B:
-                    regroup_x((u + 1) // 2, (u + 1) % 2)
+        order = []
+        for g in range(BANKS):
+            order += [(0, g), (1, g)]
+        for k in range(2, B * N // P):
+            order += [(k, g) for g in range(BANKS)]
+        done = {}
+        roots, due = {}, {}
+        ready = 0
+        f = 0
+        prepared = 2
+        for s in range(len(order)):
+            k, g = order[s]
+            square_bank(k, g)
+            u, ii, count = places[k]
+            done[u] = done.get(u, 0) + 1
+            if done[u] == BANKS * count:
+                lag = 0 if u < 2 or u == len(UNITS) - 1 else CHAIN_LAG
+                roots[s + lag] = u
+                due[s + 2 * lag] = u
+            if s in roots:
+                chain_a(roots[s])
+            if s in due:
+                chain_b(due[s])
+                ready += sum(1 for item in finals if item[0] == due[s])
+            if f < ready and k not in V_TILES:
+                final_bank(f, False, False)
+                f += 1
+            if g == BANKS - 1 and k % 4 == 1 and prepared < 2 * B and k >= 4:
+                quantise_x(prepared // 2, prepared % 2)
+                prepared += 1
+                if prepared < 2 * B:
+                    regroup_x(prepared // 2, prepared % 2)
+        while f < len(finals):
+            left = len(finals) - f
+            final_bank(f, left % 3 == 2, left <= 3)
+            f += 1

@@ -23,8 +23,11 @@ EPS = 1e-4
 FLOPS = 2 * B * O * C * N
 
 UNITS = [(0, 0, 256), (0, 256, 256), (0, 512, 512)] + [(b, h, HALF) for b in range(1, B) for h in (0, HALF)]
-V_TILES = (1, 7, 19)
-CHAIN_LAG = 2
+V_TILES = (1, 3, 7)
+LAGS = (2, 3, 4, 5, 7, 8)
+EARLY = (0, 1, 2, 2, 3, 3)
+TAIL = (1, 1, 1, 2, 3, 3)
+AHEAD = 6
 
 
 def tile_admattentionblock_pa_t_kernel(tc, x, v_qkv, g_qkv, out):
@@ -52,10 +55,9 @@ def tile_admattentionblock_pa_t_kernel(tc, x, v_qkv, g_qkv, out):
                 x_raw[b, n // HALF] = xr[:, :, n - n0:n - n0 + HALF]
 
         with tc.manual_schedule():
-            for j in range(0, 6, 2):
-                load_v(j, j + 2)
+            for j0, j1 in ((0, 1), (1, 2), (2, 4), (4, 6), (6, 8)):
+                load_v(j0, j1)
             load_x(0, 0, HALF)
-            load_v(6, 8)
             load_v(8, 12)
             load_x(0, HALF, N)
             for b in range(1, B):
@@ -99,17 +101,14 @@ def tile_admattentionblock_pa_t_kernel(tc, x, v_qkv, g_qkv, out):
         wc = keep.tile([P, O], U32, align_bytes=64)
         ws = keep.tile([P, O], U8, align_bytes=64)
 
-        def norms(pair):
-            for j in (2 * pair, 2 * pair + 1):
-                if pair == 1:
-                    junk_v = work.tile([P, C], F32, tag="junk_v", name="junk_v")
-                    nc.vector.scalar_tensor_tensor(out=junk_v[:], in0=v_sb[:, j, :], scalar=1.0,
-                                                   in1=v_sb[:, j, :], op0=ALU.mult, op1=ALU.mult,
-                                                   accum_out=ss[:, j:j + 1])
-                else:
-                    junk_s = work.tile([P, C], BF16, tag="junk_s", name="junk_s")
-                    nc.scalar.activation(out=junk_s[:], in_=v_sb[:, j, :], func=ACT.Square,
-                                         accum_out=ss[:, j:j + 1])
+        def norm_s(j):
+            junk_s = work.tile([P, C], BF16, tag="junk_s", name="junk_s")
+            nc.scalar.activation(out=junk_s[:], in_=v_sb[:, j, :], func=ACT.Square, accum_out=ss[:, j:j + 1])
+
+        def norm_v(j):
+            junk_v = work.tile([P, C], F32, tag="junk_v", name="junk_v")
+            nc.vector.scalar_tensor_tensor(out=junk_v[:], in0=v_sb[:, j, :], scalar=1.0, in1=v_sb[:, j, :],
+                                           op0=ALU.mult, op1=ALU.mult, accum_out=ss[:, j:j + 1])
 
         def root(pair):
             two = slice(2 * pair, 2 * pair + 2)
@@ -117,9 +116,11 @@ def tile_admattentionblock_pa_t_kernel(tc, x, v_qkv, g_qkv, out):
 
         wts = {}
 
-        def scale_and_turn(pair):
+        def recip(pair):
             two = slice(2 * pair, 2 * pair + 2)
             nc.vector.reciprocal(out=rnorm[:, two], in_=norm[:, two])
+
+        def scale_and_turn(pair):
             wts[pair] = psum.tile([P, 2, 2, P], F32, tag="mm", bufs=4, name="wt")
             for jj in range(2):
                 j = 2 * pair + jj
@@ -142,31 +143,43 @@ def tile_admattentionblock_pa_t_kernel(tc, x, v_qkv, g_qkv, out):
 
         on_s, on_v = nc.scalar.copy, nc.vector.tensor_copy
         with tc.manual_schedule():
-            norms(0)
+            norm_s(0)
+            norm_s(1)
             root(0)
-            norms(1)
-            scale_and_turn(0)
-            norms(2)
+            norm_v(2)
+            norm_v(3)
+            norm_s(4)
             root(1)
+            norm_s(5)
+            recip(0)
+            scale_and_turn(0)
+            recip(1)
+            norm_s(6)
             root(2)
+            norm_s(7)
             scale_and_turn(1)
             regroup_x(0, 0)
-            norms(3)
+            norm_s(8)
             root(3)
+            norm_s(9)
+            recip(2)
+            recip(3)
             scale_and_turn(2)
-            norms(4)
-            root(4)
             scale_and_turn(3)
+            norm_s(10)
+            root(4)
+            norm_s(11)
             quantise_x(0, 0)
-            gather_w(0, on_s)
+            recip(4)
+            gather_w(0, on_v)
             scale_and_turn(4)
-            norms(5)
             root(5)
-            gather_w(1, on_v)
-            quantise_w(0)
-            scale_and_turn(5)
+            gather_w(1, on_s)
             gather_w(2, on_s)
+            quantise_w(0)
+            recip(5)
             quantise_w(1)
+            scale_and_turn(5)
             gather_w(3, on_v)
             gather_w(4, on_s)
             quantise_w(2)
@@ -174,12 +187,9 @@ def tile_admattentionblock_pa_t_kernel(tc, x, v_qkv, g_qkv, out):
             quantise_w(3)
             quantise_w(4)
             quantise_w(5)
-            regroup_x(0, 1)
-        quantise_x(0, 1)
-        regroup_x(1, 0)
 
         inv_sqrt_o = 1.0 / math.sqrt(O)
-        rb, accs, mss, sts, rinvs = {}, {}, {}, {}, {}
+        rb, accs, mss, mvs, sts, rmss, rmes, rinvs = {}, {}, {}, {}, {}, {}, {}, {}
 
         def mx(ps, lw, lcols, rw, rcols):
             nc.tensor.matmul_mx(out=ps, lhsT=lw[0][:, lcols].bitcast(FP8X4), lhsT_scale=lw[1][:, lcols],
@@ -208,39 +218,57 @@ def tile_admattentionblock_pa_t_kernel(tc, x, v_qkv, g_qkv, out):
                     sts[k] = work.tile([P, BANKS, 6], F32, tag="st", name="st")
                 nc.vector.bn_stats(out=sts[k][:, g, :], in_=ps[:])
                 if g == BANKS - 1:
-                    mv = work.tile([P, 2], F32, tag="mv")
-                    nc.vector.bn_aggr(out=mv[:], in_=sts[k][:].rearrange("p g s -> p (g s)"))
-                    nc.vector.scalar_tensor_tensor(out=mss[u][:, ii:ii + 1], in0=mv[:, 0:1],
-                                                   scalar=mv[:, 0:1], in1=mv[:, 1:2],
-                                                   op0=ALU.mult, op1=ALU.add)
+                    mvs[u] = work.tile([P, 2], F32, tag="mv", name="mv")
+                    nc.vector.bn_aggr(out=mvs[u][:], in_=sts[k][:].rearrange("p g s -> p (g s)"))
             else:
                 junk = work.tile([P, HALF], BF16, tag="junk")
                 nc.scalar.activation(out=junk[:], in_=ps[:], func=ACT.Square, scale=inv_sqrt_o,
                                      accum_out=accs[u][:, BANKS * ii + g:BANKS * ii + g + 1])
-                if g == BANKS - 1 and (ii == count - 1 or (k + 1) in V_TILES):
-                    nc.vector.tensor_reduce(
-                        out=mss[u][:, 0:ii + 1],
-                        in_=accs[u][:, 0:BANKS * (ii + 1)].rearrange("p (i g) -> p i g", g=BANKS),
-                        axis=AX.X, op=ALU.add)
 
-        def chain_a(u):
-            count = UNITS[u][2] // P
-            rms = work.tile([P, 4], F32, tag="rms")
+        def on_scalar(u):
+            b, n0, width = UNITS[u]
+            last = (N * b + n0 + width) // P - 1
+            return width // P - (1 if last in V_TILES else 0)
+
+        def total(u):
+            count = on_scalar(u)
+            nc.vector.tensor_reduce(out=mss[u][:, 0:count],
+                                    in_=accs[u][:, 0:BANKS * count].rearrange("p (i g) -> p i g", g=BANKS),
+                                    axis=AX.X, op=ALU.add)
+
+        def root_rms(u):
+            count, every = on_scalar(u), UNITS[u][2] // P
+            rms = work.tile([P, 4], F32, tag="rms", name="rms")
             nc.scalar.activation(out=rms[:, 0:count], in_=mss[u][:, 0:count], func=ACT.Sqrt)
-            rme = work.tile([P, 4], F32, tag="rme")
-            nc.vector.tensor_scalar_add(out=rme[:, 0:count], in0=rms[:, 0:count], scalar1=EPS)
-            rinvs[u] = work.tile([P, 4], F32, tag="rinv", name="rinv")
-            nc.vector.reciprocal(out=rinvs[u][:, 0:count], in_=rme[:, 0:count])
+            if count < every:
+                mean, var = mvs[u][:, 0:1], mvs[u][:, 1:2]
+                nc.scalar.activation(out=rms[:, count:every], in_=mean, func=ACT.Sqrt, scale=mean, bias=var)
+            rmss[u] = rms
 
-        def chain_b(u):
+        def add_eps(u):
+            every = UNITS[u][2] // P
+            rmes[u] = work.tile([P, 4], F32, tag="rme", name="rme")
+            nc.scalar.add(out=rmes[u][:, 0:every], in_=rmss[u][:, 0:every], add=EPS)
+
+        def invert(u):
+            every = UNITS[u][2] // P
+            rinvs[u] = work.tile([P, 4], F32, tag="rinv", name="rinv")
+            nc.vector.reciprocal(out=rinvs[u][:, 0:every], in_=rmes[u][:, 0:every])
+
+        bcs = {}
+
+        def spread(u):
             width = UNITS[u][2]
-            bc = psum.tile([P, HALF], F32, tag="bc", bufs=1)
+            bc = bcs[u] = psum.tile([P, HALF], F32, tag="bc", bufs=1, name="bc")
             for q in range(width // P):
                 nc.tensor.transpose(out=bc[:, P * q:P * (q + 1)],
                                     in_=rinvs[u][:, q:q + 1].to_broadcast([P, P]),
                                     identity=ident[:])
+
+        def keep_rb(u):
+            width = UNITS[u][2]
             rb[u] = work.tile([P, HALF], F32, tag="rb", bufs=4, name="rb")
-            nc.scalar.copy(out=rb[u][:, 0:width], in_=bc[:, 0:width])
+            nc.scalar.copy(out=rb[u][:, 0:width], in_=bcs[u][:, 0:width])
 
         finals = []
         for u, (b, n0, width) in enumerate(UNITS):
@@ -276,39 +304,54 @@ def tile_admattentionblock_pa_t_kernel(tc, x, v_qkv, g_qkv, out):
             elif jj + per == group:
                 nc.sync.dma_start(out=o_view[:, j0:j0 + group, cols], in_=ot)
 
-        order = []
-        for g in range(BANKS):
-            order += [(0, g), (1, g)]
-        for k in range(2, B * N // P):
-            order += [(k, g) for g in range(BANKS)]
-        done = {}
-        roots, due = {}, {}
+        s_list = [(k, g) for k in range(B * N // P) if k not in V_TILES for g in range(BANKS)]
+        v_list = [(1, g) for g in range(BANKS)] + [None] * 3
+        v_list += list(range(0, 3)) + [(3, g) for g in range(BANKS)] + list(range(3, 6)) + [(7, g) for g in range(BANKS)]
+        v_list += list(range(6, len(finals)))
+        steps = (total, root_rms, add_eps, invert, spread, keep_rb)
+        plan = {}
+        open_banks = {u: BANKS * (width // P) for u, (b, n0, width) in enumerate(UNITS)}
+
+        def squared(k, r):
+            u = places[k][0]
+            open_banks[u] -= 1
+            if open_banks[u] == 0:
+                for step, lag in zip(steps, EARLY if u < 2 else TAIL if u == len(UNITS) - 1 else LAGS):
+                    plan.setdefault(r + lag, []).append((step, u))
+
         ready = 0
+        prepared = 1
         f = 0
-        prepared = 2
-        for s in range(len(order)):
-            k, g = order[s]
-            square_bank(k, g)
-            u, ii, count = places[k]
-            done[u] = done.get(u, 0) + 1
-            if done[u] == BANKS * count:
-                lag = 0 if u < 2 or u == len(UNITS) - 1 else CHAIN_LAG
-                roots[s + lag] = u
-                due[s + 2 * lag] = u
-            if s in roots:
-                chain_a(roots[s])
-            if s in due:
-                chain_b(due[s])
-                ready += sum(1 for item in finals if item[0] == due[s])
-            if f < ready and k not in V_TILES:
-                final_bank(f, False, False)
+        with tc.manual_schedule():
+            for r in range(len(s_list) + TAIL[-1] + 1):
+                if r < len(s_list):
+                    k, g = s_list[r]
+                    square_bank(k, g)
+                    squared(k, r)
+                item = v_list[f] if f < len(v_list) else None
+                if item is None:
+                    f += 1
+                elif isinstance(item, tuple):
+                    square_bank(item[0], item[1])
+                    squared(item[0], r)
+                    f += 1
+                elif item < ready:
+                    final_bank(item, False, False)
+                    f += 1
+                for step, u in plan.get(r, []):
+                    step(u)
+                    if step == keep_rb:
+                        ready += sum(1 for each in finals if each[0] == u)
+                if r == BANKS:
+                    regroup_x(0, 1)
+                ahead = s_list[min(r + AHEAD, len(s_list) - 1)][0]
+                if r == 5 or (r > 5 and ahead // 4 >= prepared and prepared < 2 * B):
+                    quantise_x(prepared // 2, prepared % 2)
+                    prepared += 1
+                    if prepared < 2 * B:
+                        regroup_x(prepared // 2, prepared % 2)
+            f = v_list[f] if f < len(v_list) else len(finals)
+            while f < len(finals):
+                left = len(finals) - f
+                final_bank(f, left % 3 == 2 and left < 18, left <= 3)
                 f += 1
-            if g == BANKS - 1 and k % 4 == 1 and prepared < 2 * B and k >= 4:
-                quantise_x(prepared // 2, prepared % 2)
-                prepared += 1
-                if prepared < 2 * B:
-                    regroup_x(prepared // 2, prepared % 2)
-        while f < len(finals):
-            left = len(finals) - f
-            final_bank(f, left % 3 == 2, left <= 3)
-            f += 1

@@ -23,11 +23,12 @@ EPS = 1e-4
 FLOPS = 2 * B * O * C * N
 
 UNITS = [(0, 0, 256), (0, 256, 256), (0, 512, 512)] + [(b, h, HALF) for b in range(1, B) for h in (0, HALF)]
-V_TILES = (1, 3, 7)
-LAGS = (2, 3, 4, 5, 7, 8)
-EARLY = (0, 1, 2, 2, 3, 3)
+V_TILES = (1, 6, 7)
+LAGS = (2, 3, 4, 4, 7, 7)
+EARLY = (0, 1, 1, 2, 3, 3)
 TAIL = (1, 1, 1, 2, 3, 3)
 AHEAD = 6
+HELP_AFTER = (24, 28)
 
 
 def tile_admattentionblock_pa_t_kernel(tc, x, v_qkv, g_qkv, out):
@@ -55,10 +56,11 @@ def tile_admattentionblock_pa_t_kernel(tc, x, v_qkv, g_qkv, out):
                 x_raw[b, n // HALF] = xr[:, :, n - n0:n - n0 + HALF]
 
         with tc.manual_schedule():
-            for j0, j1 in ((0, 1), (1, 2), (2, 4), (4, 6), (6, 8)):
+            for j0, j1 in ((0, 1), (1, 2), (2, 4), (4, 6)):
                 load_v(j0, j1)
             load_x(0, 0, HALF)
-            load_v(8, 12)
+            for j0, j1 in ((6, 8), (8, 10), (10, 12)):
+                load_v(j0, j1)
             load_x(0, HALF, N)
             for b in range(1, B):
                 load_x(b, 0, N)
@@ -77,9 +79,12 @@ def tile_admattentionblock_pa_t_kernel(tc, x, v_qkv, g_qkv, out):
         xgs = {}
 
         def regroup_x(b, h):
-            xg = work.tile([P, HALF, PACK], BF16, align_bytes=64, tag="xg", bufs=1, name="xg")
+            if (b, h) == (0, 0):
+                xg = keep.tile([P, HALF, PACK], BF16, align_bytes=64, name="xg0")
+            else:
+                xg = work.tile([P, HALF, PACK], BF16, align_bytes=64, tag="group", bufs=1, name="xg")
             src = x_raw[b, h]
-            if b == 0:
+            if (b, h) == (0, 0):
                 nc.vector.tensor_copy(out=xg[:].rearrange("p (c i) t -> p c t i", i=4),
                                       in_=src.rearrange("p t (c i) -> p c t i", i=4))
             else:
@@ -97,7 +102,12 @@ def tile_admattentionblock_pa_t_kernel(tc, x, v_qkv, g_qkv, out):
         norm = keep.tile([P, J], F32)
         rnorm = keep.tile([P, J], F32)
         w_bf = keep.tile([P, J, C], BF16)
-        wg = keep.tile([P, J, P, PACK], BF16, align_bytes=64)
+        wgs = [keep.tile([P, 4, P, PACK], BF16, align_bytes=64, name="wg%d" % c) for c in range(2)]
+        wgs.append(work.tile([P, 4, P, PACK], BF16, align_bytes=64, tag="group", bufs=1, name="wg2"))
+
+        def w_rows(pair):
+            return wgs[pair // 2][:, 2 * (pair % 2):2 * (pair % 2) + 2].rearrange("p j o t -> p (j o t)")
+
         wc = keep.tile([P, O], U32, align_bytes=64)
         ws = keep.tile([P, O], U8, align_bytes=64)
 
@@ -132,21 +142,21 @@ def tile_admattentionblock_pa_t_kernel(tc, x, v_qkv, g_qkv, out):
                     nc.tensor.transpose(out=wts[pair][:, jj, u, :], in_=words[:, u::2], identity=ident[:])
 
         def gather_w(pair, copy):
-            dst = wg[:, 2 * pair:2 * pair + 2].rearrange("p j o t -> p (j o t)").bitcast(F32)
+            dst = w_rows(pair).bitcast(F32)
             copy(out=dst.rearrange("p (j o u) -> p j o u", j=2, u=2),
                  in_=wts[pair][:].rearrange("p j u o -> p j o u"))
 
         def quantise_w(pair):
             cols = slice(2 * P * pair, 2 * P * (pair + 1))
             nc.vector.quantize_mx(out=wc[:, cols].bitcast(FP8X4), scales=ws[:, cols],
-                                  in_=wg[:, 2 * pair:2 * pair + 2].rearrange("p j o t -> p (j o t)"))
+                                  in_=w_rows(pair))
 
         on_s, on_v = nc.scalar.copy, nc.vector.tensor_copy
         with tc.manual_schedule():
             norm_s(0)
-            norm_s(1)
+            norm_v(1)
+            norm_s(2)
             root(0)
-            norm_v(2)
             norm_v(3)
             norm_s(4)
             root(1)
@@ -154,39 +164,40 @@ def tile_admattentionblock_pa_t_kernel(tc, x, v_qkv, g_qkv, out):
             recip(0)
             scale_and_turn(0)
             recip(1)
+            scale_and_turn(1)
             norm_s(6)
             root(2)
-            norm_s(7)
-            scale_and_turn(1)
             regroup_x(0, 0)
+            norm_s(7)
             norm_s(8)
             root(3)
-            norm_s(9)
             recip(2)
-            recip(3)
             scale_and_turn(2)
-            scale_and_turn(3)
+            norm_s(9)
             norm_s(10)
             root(4)
-            norm_s(11)
-            quantise_x(0, 0)
-            recip(4)
             gather_w(0, on_v)
-            scale_and_turn(4)
+            quantise_x(0, 0)
+            recip(3)
+            scale_and_turn(3)
+            norm_s(11)
             root(5)
-            gather_w(1, on_s)
-            gather_w(2, on_s)
             quantise_w(0)
+            gather_w(1, on_v)
+            recip(4)
+            scale_and_turn(4)
+            gather_w(2, on_s)
             recip(5)
             quantise_w(1)
             scale_and_turn(5)
-            gather_w(3, on_v)
-            gather_w(4, on_s)
+            gather_w(3, on_s)
             quantise_w(2)
-            gather_w(5, on_s)
+            gather_w(4, on_s)
             quantise_w(3)
+            gather_w(5, on_s)
             quantise_w(4)
             quantise_w(5)
+            regroup_x(0, 1)
 
         inv_sqrt_o = 1.0 / math.sqrt(O)
         rb, accs, mss, mvs, sts, rmss, rmes, rinvs = {}, {}, {}, {}, {}, {}, {}, {}
@@ -218,17 +229,20 @@ def tile_admattentionblock_pa_t_kernel(tc, x, v_qkv, g_qkv, out):
                     sts[k] = work.tile([P, BANKS, 6], F32, tag="st", name="st")
                 nc.vector.bn_stats(out=sts[k][:, g, :], in_=ps[:])
                 if g == BANKS - 1:
-                    mvs[u] = work.tile([P, 2], F32, tag="mv", name="mv")
-                    nc.vector.bn_aggr(out=mvs[u][:], in_=sts[k][:].rearrange("p g s -> p (g s)"))
+                    mvs[k] = work.tile([P, 2], F32, tag="mv", name="mv")
+                    nc.vector.bn_aggr(out=mvs[k][:], in_=sts[k][:].rearrange("p g s -> p (g s)"))
             else:
                 junk = work.tile([P, HALF], BF16, tag="junk")
                 nc.scalar.activation(out=junk[:], in_=ps[:], func=ACT.Square, scale=inv_sqrt_o,
                                      accum_out=accs[u][:, BANKS * ii + g:BANKS * ii + g + 1])
 
-        def on_scalar(u):
+        def tiles_of(u):
             b, n0, width = UNITS[u]
-            last = (N * b + n0 + width) // P - 1
-            return width // P - (1 if last in V_TILES else 0)
+            first = (N * b + n0) // P
+            return range(first, first + width // P)
+
+        def on_scalar(u):
+            return sum(1 for k in tiles_of(u) if k not in V_TILES)
 
         def total(u):
             count = on_scalar(u)
@@ -240,9 +254,10 @@ def tile_admattentionblock_pa_t_kernel(tc, x, v_qkv, g_qkv, out):
             count, every = on_scalar(u), UNITS[u][2] // P
             rms = work.tile([P, 4], F32, tag="rms", name="rms")
             nc.scalar.activation(out=rms[:, 0:count], in_=mss[u][:, 0:count], func=ACT.Sqrt)
-            if count < every:
-                mean, var = mvs[u][:, 0:1], mvs[u][:, 1:2]
-                nc.scalar.activation(out=rms[:, count:every], in_=mean, func=ACT.Sqrt, scale=mean, bias=var)
+            for ii in range(count, every):
+                mv = mvs[tiles_of(u)[ii]]
+                nc.scalar.activation(out=rms[:, ii:ii + 1], in_=mv[:, 0:1], func=ACT.Sqrt, scale=mv[:, 0:1],
+                                     bias=mv[:, 1:2])
             rmss[u] = rms
 
         def add_eps(u):
@@ -304,10 +319,14 @@ def tile_admattentionblock_pa_t_kernel(tc, x, v_qkv, g_qkv, out):
             elif jj + per == group:
                 nc.sync.dma_start(out=o_view[:, j0:j0 + group, cols], in_=ot)
 
-        s_list = [(k, g) for k in range(B * N // P) if k not in V_TILES for g in range(BANKS)]
-        v_list = [(1, g) for g in range(BANKS)] + [None] * 3
-        v_list += list(range(0, 3)) + [(3, g) for g in range(BANKS)] + list(range(3, 6)) + [(7, g) for g in range(BANKS)]
-        v_list += list(range(6, len(finals)))
+        s_list = []
+        for k in range(B * N // P):
+            if k not in V_TILES:
+                s_list += [(k, g) for g in range(BANKS)]
+            if k in HELP_AFTER:
+                s_list.append(None)
+        v_list = [(1, g) for g in range(BANKS)] + [None] * 2 + ["final"] * 6
+        v_list += [(k, g) for k in (6, 7) for g in range(BANKS)]
         steps = (total, root_rms, add_eps, invert, spread, keep_rb)
         plan = {}
         open_banks = {u: BANKS * (width // P) for u, (b, n0, width) in enumerate(UNITS)}
@@ -322,36 +341,38 @@ def tile_admattentionblock_pa_t_kernel(tc, x, v_qkv, g_qkv, out):
         ready = 0
         prepared = 1
         f = 0
+        at = 0
         with tc.manual_schedule():
             for r in range(len(s_list) + TAIL[-1] + 1):
-                if r < len(s_list):
+                if r < len(s_list) and s_list[r] is not None:
                     k, g = s_list[r]
                     square_bank(k, g)
                     squared(k, r)
-                item = v_list[f] if f < len(v_list) else None
-                if item is None:
+                elif r < len(s_list) and f < ready:
+                    final_bank(f, True, False)
                     f += 1
-                elif isinstance(item, tuple):
-                    square_bank(item[0], item[1])
-                    squared(item[0], r)
-                    f += 1
-                elif item < ready:
-                    final_bank(item, False, False)
-                    f += 1
+                item = v_list[at] if at < len(v_list) else "final"
+                if item == "final":
+                    if f < ready:
+                        final_bank(f, False, False)
+                        f += 1
+                        at += 1
+                else:
+                    at += 1
+                    if item is not None:
+                        square_bank(item[0], item[1])
+                        squared(item[0], r)
                 for step, u in plan.get(r, []):
                     step(u)
                     if step == keep_rb:
                         ready += sum(1 for each in finals if each[0] == u)
-                if r == BANKS:
-                    regroup_x(0, 1)
-                ahead = s_list[min(r + AHEAD, len(s_list) - 1)][0]
-                if r == 5 or (r > 5 and ahead // 4 >= prepared and prepared < 2 * B):
+                ahead = max(item[0] for item in s_list[0:r + AHEAD] if item is not None)
+                if r == 4 or (r > 4 and ahead // 4 >= prepared and prepared < 2 * B):
                     quantise_x(prepared // 2, prepared % 2)
                     prepared += 1
                     if prepared < 2 * B:
                         regroup_x(prepared // 2, prepared % 2)
-            f = v_list[f] if f < len(v_list) else len(finals)
             while f < len(finals):
                 left = len(finals) - f
-                final_bank(f, left % 3 == 2 and left < 18, left <= 3)
+                final_bank(f, left % 3 == 2, left <= 3)
                 f += 1

@@ -24,7 +24,7 @@ FLOPS = 2 * B * O * C * N
 
 UNITS = [(0, 0, 256), (0, 256, 256), (0, 512, 512)] + [(b, h, HALF) for b in range(1, B) for h in (0, HALF)]
 V_TILES = (1, 6, 7)
-LAGS = (2, 3, 4, 4, 7, 7)
+LAGS = (1, 2, 3, 3, 6, 6)
 EARLY = (0, 1, 1, 2, 3, 3)
 TAIL = (1, 1, 1, 2, 3, 3)
 AHEAD = 6
@@ -56,11 +56,10 @@ def tile_admattentionblock_pa_t_kernel(tc, x, v_qkv, g_qkv, out):
                 x_raw[b, n // HALF] = xr[:, :, n - n0:n - n0 + HALF]
 
         with tc.manual_schedule():
-            for j0, j1 in ((0, 1), (1, 2), (2, 4), (4, 6)):
+            for j0, j1 in ((0, 1), (1, 2), (2, 3), (3, 4), (4, 6), (6, 8), (8, 10)):
                 load_v(j0, j1)
             load_x(0, 0, HALF)
-            for j0, j1 in ((6, 8), (8, 10), (10, 12)):
-                load_v(j0, j1)
+            load_v(10, 12)
             load_x(0, HALF, N)
             for b in range(1, B):
                 load_x(b, 0, N)
@@ -74,8 +73,8 @@ def tile_admattentionblock_pa_t_kernel(tc, x, v_qkv, g_qkv, out):
         g_f = keep.tile([P, J], F32)
         nc.gpsimd.tensor_copy(out=g_f[:], in_=g_bf[:])
 
-        xc = [keep.tile([P, N], U32, align_bytes=64, name="xc%d" % b) for b in range(B)]
-        xs = [keep.tile([P, N], U8, align_bytes=64, name="xs%d" % b) for b in range(B)]
+        xc = [keep.tile([P, N], U32, align_bytes=256, name="xc%d" % b) for b in range(B)]
+        xs = [keep.tile([P, N], U8, align_bytes=256, name="xs%d" % b) for b in range(B)]
         xgs = {}
 
         def regroup_x(b, h):
@@ -108,8 +107,8 @@ def tile_admattentionblock_pa_t_kernel(tc, x, v_qkv, g_qkv, out):
         def w_rows(pair):
             return wgs[pair // 2][:, 2 * (pair % 2):2 * (pair % 2) + 2].rearrange("p j o t -> p (j o t)")
 
-        wc = keep.tile([P, O], U32, align_bytes=64)
-        ws = keep.tile([P, O], U8, align_bytes=64)
+        wc = keep.tile([P, O], U32, align_bytes=256)
+        ws = keep.tile([P, O], U8, align_bytes=256)
 
         def norm_s(j):
             junk_s = work.tile([P, C], BF16, tag="junk_s", name="junk_s")
@@ -160,37 +159,37 @@ def tile_admattentionblock_pa_t_kernel(tc, x, v_qkv, g_qkv, out):
             norm_v(3)
             norm_s(4)
             root(1)
-            norm_s(5)
             recip(0)
             scale_and_turn(0)
+            norm_s(6)
+            norm_v(5)
+            root(2)
+            norm_s(7)
             recip(1)
             scale_and_turn(1)
-            norm_s(6)
-            root(2)
-            regroup_x(0, 0)
-            norm_s(7)
             norm_s(8)
             root(3)
+            norm_s(9)
             recip(2)
             scale_and_turn(2)
-            norm_s(9)
-            norm_s(10)
-            root(4)
             gather_w(0, on_v)
-            quantise_x(0, 0)
+            gather_w(1, on_s)
+            regroup_x(0, 0)
+            norm_s(10)
+            norm_s(11)
+            root(4)
+            root(5)
             recip(3)
             scale_and_turn(3)
-            norm_s(11)
-            root(5)
-            quantise_w(0)
-            gather_w(1, on_v)
             recip(4)
-            scale_and_turn(4)
-            gather_w(2, on_s)
             recip(5)
-            quantise_w(1)
+            scale_and_turn(4)
             scale_and_turn(5)
+            gather_w(2, on_s)
             gather_w(3, on_s)
+            quantise_w(0)
+            quantise_x(0, 0)
+            quantise_w(1)
             quantise_w(2)
             gather_w(4, on_s)
             quantise_w(3)

@@ -28,6 +28,9 @@ LAGS = (1, 2, 3, 3, 6, 6)
 EARLY = (0, 1, 1, 2, 3, 3)
 TAIL = (1, 1, 1, 2, 3, 3)
 AHEAD = 6
+ALONE = 2
+STORE_LAG = 2
+HELP_PHASE = 1
 HELP_AFTER = (24, 28)
 
 
@@ -181,6 +184,7 @@ def tile_admattentionblock_pa_t_kernel(tc, x, v_qkv, g_qkv, out):
             root(5)
             recip(3)
             scale_and_turn(3)
+            quantise_x(0, 0)
             recip(4)
             recip(5)
             scale_and_turn(4)
@@ -188,7 +192,6 @@ def tile_admattentionblock_pa_t_kernel(tc, x, v_qkv, g_qkv, out):
             gather_w(2, on_s)
             gather_w(3, on_s)
             quantise_w(0)
-            quantise_x(0, 0)
             quantise_w(1)
             quantise_w(2)
             gather_w(4, on_s)
@@ -293,7 +296,9 @@ def tile_admattentionblock_pa_t_kernel(tc, x, v_qkv, g_qkv, out):
                     finals.append((u, j0, jj, per, group))
         ots = {}
 
-        def final_bank(f, helped, alone):
+        late, by_itself = {}, set()
+
+        def final_bank(f, helped, alone, round_now):
             u, j0, jj, per, group = finals[f]
             b, n0, width = UNITS[u]
             cols = slice(n0, n0 + width)
@@ -313,10 +318,14 @@ def tile_admattentionblock_pa_t_kernel(tc, x, v_qkv, g_qkv, out):
                 nc.gpsimd.tensor_tensor(out=dst, in0=dst, in1=r, op=ALU.mult)
             else:
                 nc.vector.tensor_tensor(out=dst, in0=ps, in1=r, op=ALU.mult)
-            if alone:
+            if helped:
+                late.setdefault(round_now + STORE_LAG, []).append((o_view[:, j0:j0 + per, cols], dst))
+                by_itself.add((u, j0))
+            elif alone:
                 nc.sync.dma_start(out=o_view[:, j0 + jj:j0 + jj + per, cols], in_=dst)
             elif jj + per == group:
-                nc.sync.dma_start(out=o_view[:, j0:j0 + group, cols], in_=ot)
+                first = per if (u, j0) in by_itself else 0
+                nc.sync.dma_start(out=o_view[:, j0 + first:j0 + group, cols], in_=ot[:, first:group, :])
 
         s_list = []
         for k in range(B * N // P):
@@ -339,22 +348,32 @@ def tile_admattentionblock_pa_t_kernel(tc, x, v_qkv, g_qkv, out):
 
         ready = 0
         prepared = 1
-        f = 0
+        taken = set()
         at = 0
+
+        def next_final(first_of_group):
+            for i in range(ready):
+                if i not in taken and (finals[i][2] == 0 or not first_of_group):
+                    taken.add(i)
+                    return i
+            return None
+
         with tc.manual_schedule():
-            for r in range(len(s_list) + TAIL[-1] + 1):
+            r = 0
+            while len(taken) < len(finals) or any(each >= r for each in late):
                 if r < len(s_list) and s_list[r] is not None:
                     k, g = s_list[r]
                     square_bank(k, g)
                     squared(k, r)
-                elif r < len(s_list) and f < ready:
-                    final_bank(f, True, False)
-                    f += 1
+                elif r < len(s_list) or r % 2 == HELP_PHASE:
+                    i = next_final(True)
+                    if i is not None:
+                        final_bank(i, True, False, r)
                 item = v_list[at] if at < len(v_list) else "final"
                 if item == "final":
-                    if f < ready:
-                        final_bank(f, False, False)
-                        f += 1
+                    i = next_final(False)
+                    if i is not None:
+                        final_bank(i, False, i >= len(finals) - ALONE, r)
                         at += 1
                 else:
                     at += 1
@@ -365,13 +384,12 @@ def tile_admattentionblock_pa_t_kernel(tc, x, v_qkv, g_qkv, out):
                     step(u)
                     if step == keep_rb:
                         ready += sum(1 for each in finals if each[0] == u)
+                for view, tile in late.get(r, []):
+                    nc.sync.dma_start(out=view, in_=tile)
                 ahead = max(item[0] for item in s_list[0:r + AHEAD] if item is not None)
                 if r == 4 or (r > 4 and ahead // 4 >= prepared and prepared < 2 * B):
                     quantise_x(prepared // 2, prepared % 2)
                     prepared += 1
                     if prepared < 2 * B:
                         regroup_x(prepared // 2, prepared % 2)
-            while f < len(finals):
-                left = len(finals) - f
-                final_bank(f, left % 3 == 2, left <= 3)
-                f += 1
+                r += 1

@@ -24,8 +24,8 @@ FLOPS = 2 * B * O * C * N
 
 UNITS = [(0, 0, 256), (0, 256, 256), (0, 512, 512)] + [(b, h, HALF) for b in range(1, B) for h in (0, HALF)]
 V_TILES = (1, 6, 7)
-LAGS = (1, 2, 3, 3, 6, 6)
-EARLY = (0, 1, 1, 2, 3, 3)
+LAGS = (1, 3, 3, 3, 6, 6)
+EARLY = (0, 1, 1, 1, 3, 3)
 TAIL = (1, 1, 1, 2, 3, 3)
 AHEAD = 6
 ALONE = 2
@@ -184,7 +184,6 @@ def tile_admattentionblock_pa_t_kernel(tc, x, v_qkv, g_qkv, out):
             root(5)
             recip(3)
             scale_and_turn(3)
-            quantise_x(0, 0)
             recip(4)
             recip(5)
             scale_and_turn(4)
@@ -192,6 +191,7 @@ def tile_admattentionblock_pa_t_kernel(tc, x, v_qkv, g_qkv, out):
             gather_w(2, on_s)
             gather_w(3, on_s)
             quantise_w(0)
+            quantise_x(0, 0)
             quantise_w(1)
             quantise_w(2)
             gather_w(4, on_s)

@@ -24,7 +24,7 @@ FLOPS = 2 * B * O * C * N
 
 UNITS = [(0, 0, 256), (0, 256, 256), (0, 512, 512)] + [(b, h, HALF) for b in range(1, B) for h in (0, HALF)]
 V_TILES = (1, 6, 7)
-LAGS = (1, 3, 3, 3, 6, 6)
+LAGS = (1, 2, 3, 3, 6, 6)
 EARLY = (0, 1, 1, 1, 3, 3)
 TAIL = (1, 1, 1, 2, 3, 3)
 AHEAD = 6
@@ -358,7 +358,7 @@ def tile_admattentionblock_pa_t_kernel(tc, x, v_qkv, g_qkv, out):
                     return i
             return None
 
-        with tc.manual_schedule():
+        if True:
             r = 0
             while len(taken) < len(finals) or any(each >= r for each in late):
                 if r < len(s_list) and s_list[r] is not None:

from contextlib import ExitStack
import math

import concourse.mybir as mybir
from concourse.masks import make_identity

F32 = mybir.dt.float32
BF16 = mybir.dt.bfloat16
U32 = mybir.dt.uint32
U8 = mybir.dt.uint8
FP8X4 = mybir.dt.float8_e4m3fn_x4
ACT = mybir.ActivationFunctionType
ALU = mybir.AluOpType
AX = mybir.AxisListType

B, C, N, O = 4, 512, 1024, 1536
P = 128
PACK = 4
J = O // P
HALF = 512
BANKS = O // HALF
EPS = 1e-4
FLOPS = 2 * B * O * C * N

UNITS = [(0, 0, 256), (0, 256, 256), (0, 512, 512)] + [(b, h, HALF) for b in range(1, B) for h in (0, HALF)]
V_TILES = (1, 6, 7)
LAGS = (1, 2, 3, 3, 6, 6)
EARLY = (0, 1, 1, 1, 3, 3)
TAIL = (1, 1, 1, 2, 3, 3)
AHEAD = 6
ALONE = 2
STORE_LAG = 2
HELP_PHASE = 1
HELP_AFTER = (24, 28)


def tile_admattentionblock_pa_t_kernel(tc, x, v_qkv, g_qkv, out):
    nc = tc.nc
    with ExitStack() as ctx:
        keep = ctx.enter_context(tc.tile_pool(name="keep", bufs=1))
        work = ctx.enter_context(tc.tile_pool(name="work", bufs=2))
        stage = ctx.enter_context(tc.tile_pool(name="stage", bufs=8))
        psum = ctx.enter_context(tc.psum_pool(name="psum", bufs=1))

        g_bf = keep.tile([P, J], BF16)
        nc.scalar.dma_start(out=g_bf[:], in_=g_qkv.rearrange("(p j) -> p j", j=J))
        v_sb = keep.tile([P, J, C], BF16)
        v_view = v_qkv.rearrange("(p j) c -> p j c", j=J)
        x_raw = {}

        def load_v(j0, j1):
            nc.sync.dma_start(out=v_sb[:, j0:j1, :], in_=v_view[:, j0:j1, :])

        def load_x(b, n0, n1):
            view = x[b].rearrange("(p t) h w -> p t (h w)", t=PACK)
            xr = keep.tile([P, PACK, n1 - n0], BF16, name="x_raw%d_%d" % (b, n0))
            nc.sync.dma_start(out=xr[:], in_=view[:, :, n0:n1])
            for n in range(n0, n1, HALF):
                x_raw[b, n // HALF] = xr[:, :, n - n0:n - n0 + HALF]

        with tc.manual_schedule():
            for j0, j1 in ((0, 1), (1, 2), (2, 3), (3, 4), (4, 6), (6, 8), (8, 10)):
                load_v(j0, j1)
            load_x(0, 0, HALF)
            load_v(10, 12)
            load_x(0, HALF, N)
            for b in range(1, B):
                load_x(b, 0, N)

        ident = keep.tile([P, P], F32)
        make_identity(nc, ident[:])
        one = keep.tile([P, 1], F32)
        nc.vector.memset(one[:], 1.0)
        warm = keep.tile([P, 1], F32)
        nc.scalar.activation(out=warm[:], in_=one[:], func=ACT.Sqrt)
        g_f = keep.tile([P, J], F32)
        nc.gpsimd.tensor_copy(out=g_f[:], in_=g_bf[:])

        xc = [keep.tile([P, N], U32, align_bytes=256, name="xc%d" % b) for b in range(B)]
        xs = [keep.tile([P, N], U8, align_bytes=256, name="xs%d" % b) for b in range(B)]
        xgs = {}

        def regroup_x(b, h):
            if (b, h) == (0, 0):
                xg = keep.tile([P, HALF, PACK], BF16, align_bytes=64, name="xg0")
            else:
                xg = work.tile([P, HALF, PACK], BF16, align_bytes=64, tag="group", bufs=1, name="xg")
            src = x_raw[b, h]
            if (b, h) == (0, 0):
                nc.vector.tensor_copy(out=xg[:].rearrange("p (c i) t -> p c t i", i=4),
                                      in_=src.rearrange("p t (c i) -> p c t i", i=4))
            else:
                nc.gpsimd.tensor_scalar(out=xg[:], in0=src.rearrange("p t n -> p n t"),
                                        scalar1=1.0, scalar2=0.0, op0=ALU.mult, op1=ALU.add)
            xgs[(b, h)] = xg

        def quantise_x(b, h):
            nc.vector.quantize_mx(
                out=xc[b][:, HALF * h:HALF * (h + 1)].bitcast(FP8X4),
                scales=xs[b][:, HALF * h:HALF * (h + 1)],
                in_=xgs[(b, h)][:].rearrange("p n t -> p (n t)"))

        ss = keep.tile([P, J], F32)
        norm = keep.tile([P, J], F32)
        rnorm = keep.tile([P, J], F32)
        w_bf = keep.tile([P, J, C], BF16)
        wgs = [keep.tile([P, 4, P, PACK], BF16, align_bytes=64, name="wg%d" % c) for c in range(2)]
        wgs.append(work.tile([P, 4, P, PACK], BF16, align_bytes=64, tag="group", bufs=1, name="wg2"))

        def w_rows(pair):
            return wgs[pair // 2][:, 2 * (pair % 2):2 * (pair % 2) + 2].rearrange("p j o t -> p (j o t)")

        wc = keep.tile([P, O], U32, align_bytes=256)
        ws = keep.tile([P, O], U8, align_bytes=256)

        def norm_s(j):
            junk_s = work.tile([P, C], BF16, tag="junk_s", name="junk_s")
            nc.scalar.activation(out=junk_s[:], in_=v_sb[:, j, :], func=ACT.Square, accum_out=ss[:, j:j + 1])

        def norm_v(j):
            junk_v = work.tile([P, C], F32, tag="junk_v", name="junk_v")
            nc.vector.scalar_tensor_tensor(out=junk_v[:], in0=v_sb[:, j, :], scalar=1.0, in1=v_sb[:, j, :],
                                           op0=ALU.mult, op1=ALU.mult, accum_out=ss[:, j:j + 1])

        def root(pair):
            two = slice(2 * pair, 2 * pair + 2)
            nc.scalar.activation(out=norm[:, two], in_=ss[:, two], func=ACT.Sqrt)

        wts = {}

        def recip(pair):
            two = slice(2 * pair, 2 * pair + 2)
            nc.vector.reciprocal(out=rnorm[:, two], in_=norm[:, two])

        def scale_and_turn(pair):
            wts[pair] = psum.tile([P, 2, 2, P], F32, tag="mm", bufs=4, name="wt")
            for jj in range(2):
                j = 2 * pair + jj
                nc.vector.tensor_scalar(out=w_bf[:, j, :], in0=v_sb[:, j, :],
                                        scalar1=rnorm[:, j:j + 1], scalar2=g_f[:, j:j + 1],
                                        op0=ALU.mult, op1=ALU.mult)
                words = w_bf[:, j, :].bitcast(F32)
                for u in range(2):
                    nc.tensor.transpose(out=wts[pair][:, jj, u, :], in_=words[:, u::2], identity=ident[:])

        def gather_w(pair, copy):
            dst = w_rows(pair).bitcast(F32)
            copy(out=dst.rearrange("p (j o u) -> p j o u", j=2, u=2),
                 in_=wts[pair][:].rearrange("p j u o -> p j o u"))

        def quantise_w(pair):
            cols = slice(2 * P * pair, 2 * P * (pair + 1))
            nc.vector.quantize_mx(out=wc[:, cols].bitcast(FP8X4), scales=ws[:, cols],
                                  in_=w_rows(pair))

        on_s, on_v = nc.scalar.copy, nc.vector.tensor_copy
        with tc.manual_schedule():
            norm_s(0)
            norm_v(1)
            norm_s(2)
            root(0)
            norm_v(3)
            norm_s(4)
            root(1)
            recip(0)
            scale_and_turn(0)
            norm_s(6)
            norm_v(5)
            root(2)
            norm_s(7)
            recip(1)
            scale_and_turn(1)
            norm_s(8)
            root(3)
            norm_s(9)
            recip(2)
            scale_and_turn(2)
            gather_w(0, on_v)
            gather_w(1, on_s)
            regroup_x(0, 0)
            norm_s(10)
            norm_s(11)
            root(4)
            root(5)
            recip(3)
            scale_and_turn(3)
            recip(4)
            recip(5)
            scale_and_turn(4)
            scale_and_turn(5)
            gather_w(2, on_s)
            gather_w(3, on_s)
            quantise_w(0)
            quantise_x(0, 0)
            quantise_w(1)
            quantise_w(2)
            gather_w(4, on_s)
            quantise_w(3)
            gather_w(5, on_s)
            quantise_w(4)
            quantise_w(5)
            regroup_x(0, 1)

        inv_sqrt_o = 1.0 / math.sqrt(O)
        rb, accs, mss, mvs, sts, rmss, rmes, rinvs = {}, {}, {}, {}, {}, {}, {}, {}

        def mx(ps, lw, lcols, rw, rcols):
            nc.tensor.matmul_mx(out=ps, lhsT=lw[0][:, lcols].bitcast(FP8X4), lhsT_scale=lw[1][:, lcols],
                                rhs=rw[0][:, rcols].bitcast(FP8X4), rhs_scale=rw[1][:, rcols],
                                start=True, stop=True)

        places = []
        for u, (b, n0, width) in enumerate(UNITS):
            for ii in range(width // P):
                places.append((u, ii, width // P))

        def square_bank(k, g):
            b, i = divmod(k, N // P)
            u, ii, count = places[k]
            if u not in accs:
                accs[u] = work.tile([P, 4 * BANKS], F32, tag="acc", name="acc")
                mss[u] = work.tile([P, 4], F32, tag="ms", name="ms")
            on_vector = k in V_TILES
            if on_vector:
                ps = psum.tile([P, HALF], F32, tag="mm", bufs=4, name="ps_sv")
            else:
                ps = psum.tile([P, HALF], F32, tag="sq", bufs=3, name="ps_sq")
            mx(ps[:], (xc[b], xs[b]), slice(P * i, P * (i + 1)), (wc, ws), slice(HALF * g, HALF * (g + 1)))
            if on_vector:
                if g == 0:
                    sts[k] = work.tile([P, BANKS, 6], F32, tag="st", name="st")
                nc.vector.bn_stats(out=sts[k][:, g, :], in_=ps[:])
                if g == BANKS - 1:
                    mvs[k] = work.tile([P, 2], F32, tag="mv", name="mv")
                    nc.vector.bn_aggr(out=mvs[k][:], in_=sts[k][:].rearrange("p g s -> p (g s)"))
            else:
                junk = work.tile([P, HALF], BF16, tag="junk")
                nc.scalar.activation(out=junk[:], in_=ps[:], func=ACT.Square, scale=inv_sqrt_o,
                                     accum_out=accs[u][:, BANKS * ii + g:BANKS * ii + g + 1])

        def tiles_of(u):
            b, n0, width = UNITS[u]
            first = (N * b + n0) // P
            return range(first, first + width // P)

        def on_scalar(u):
            return sum(1 for k in tiles_of(u) if k not in V_TILES)

        def total(u):
            count = on_scalar(u)
            nc.vector.tensor_reduce(out=mss[u][:, 0:count],
                                    in_=accs[u][:, 0:BANKS * count].rearrange("p (i g) -> p i g", g=BANKS),
                                    axis=AX.X, op=ALU.add)

        def root_rms(u):
            count, every = on_scalar(u), UNITS[u][2] // P
            rms = work.tile([P, 4], F32, tag="rms", name="rms")
            nc.scalar.activation(out=rms[:, 0:count], in_=mss[u][:, 0:count], func=ACT.Sqrt)
            for ii in range(count, every):
                mv = mvs[tiles_of(u)[ii]]
                nc.scalar.activation(out=rms[:, ii:ii + 1], in_=mv[:, 0:1], func=ACT.Sqrt, scale=mv[:, 0:1],
                                     bias=mv[:, 1:2])
            rmss[u] = rms

        def add_eps(u):
            every = UNITS[u][2] // P
            rmes[u] = work.tile([P, 4], F32, tag="rme", name="rme")
            nc.scalar.add(out=rmes[u][:, 0:every], in_=rmss[u][:, 0:every], add=EPS)

        def invert(u):
            every = UNITS[u][2] // P
            rinvs[u] = work.tile([P, 4], F32, tag="rinv", name="rinv")
            nc.vector.reciprocal(out=rinvs[u][:, 0:every], in_=rmes[u][:, 0:every])

        bcs = {}

        def spread(u):
            width = UNITS[u][2]
            bc = bcs[u] = psum.tile([P, HALF], F32, tag="bc", bufs=1, name="bc")
            for q in range(width // P):
                nc.tensor.transpose(out=bc[:, P * q:P * (q + 1)],
                                    in_=rinvs[u][:, q:q + 1].to_broadcast([P, P]),
                                    identity=ident[:])

        def keep_rb(u):
            width = UNITS[u][2]
            rb[u] = work.tile([P, HALF], F32, tag="rb", bufs=4, name="rb")
            nc.scalar.copy(out=rb[u][:, 0:width], in_=bcs[u][:, 0:width])

        finals = []
        for u, (b, n0, width) in enumerate(UNITS):
            per = HALF // width
            group = 4 if width == 256 else 3
            for j0 in range(0, J, group):
                for jj in range(0, group, per):
                    finals.append((u, j0, jj, per, group))
        ots = {}

        late, by_itself = {}, set()

        def final_bank(f, helped, alone, round_now):
            u, j0, jj, per, group = finals[f]
            b, n0, width = UNITS[u]
            cols = slice(n0, n0 + width)
            o_view = out[b].rearrange("(p j) n -> p j n", j=J)
            if jj == 0:
                ots[u, j0] = stage.tile([P, 3 * HALF], F32, tag="ot", name="ot")
            ot = ots[u, j0][:, 0:group * width].rearrange("p (j n) -> p j n", j=group)
            dst = ot[:, jj:jj + per, :]
            ps = psum.tile([P, HALF], F32, tag="mm", bufs=4, name="ps_mm")
            ps = ps[:].rearrange("p (j n) -> p j n", j=per)
            for e in range(per):
                j = j0 + jj + e
                mx(ps[:, e, :], (wc, ws), slice(P * j, P * (j + 1)), (xc[b], xs[b]), cols)
            r = rb[u][:, 0:width].unsqueeze(1).to_broadcast([P, per, width])
            if helped:
                nc.scalar.copy(out=dst, in_=ps)
                nc.gpsimd.tensor_tensor(out=dst, in0=dst, in1=r, op=ALU.mult)
            else:
                nc.vector.tensor_tensor(out=dst, in0=ps, in1=r, op=ALU.mult)
            if helped:
                late.setdefault(round_now + STORE_LAG, []).append((o_view[:, j0:j0 + per, cols], dst))
                by_itself.add((u, j0))
            elif alone:
                nc.sync.dma_start(out=o_view[:, j0 + jj:j0 + jj + per, cols], in_=dst)
            elif jj + per == group:
                first = per if (u, j0) in by_itself else 0
                nc.sync.dma_start(out=o_view[:, j0 + first:j0 + group, cols], in_=ot[:, first:group, :])

        s_list = []
        for k in range(B * N // P):
            if k not in V_TILES:
                s_list += [(k, g) for g in range(BANKS)]
            if k in HELP_AFTER:
                s_list.append(None)
        v_list = [(1, g) for g in range(BANKS)] + [None] * 2 + ["final"] * 6
        v_list += [(k, g) for k in (6, 7) for g in range(BANKS)]
        steps = (total, root_rms, add_eps, invert, spread, keep_rb)
        plan = {}
        open_banks = {u: BANKS * (width // P) for u, (b, n0, width) in enumerate(UNITS)}

        def squared(k, r):
            u = places[k][0]
            open_banks[u] -= 1
            if open_banks[u] == 0:
                for step, lag in zip(steps, EARLY if u < 2 else TAIL if u == len(UNITS) - 1 else LAGS):
                    plan.setdefault(r + lag, []).append((step, u))

        ready = 0
        prepared = 1
        taken = set()
        at = 0

        def next_final(first_of_group):
            for i in range(ready):
                if i not in taken and (finals[i][2] == 0 or not first_of_group):
                    taken.add(i)
                    return i
            return None

        if True:
            r = 0
            while len(taken) < len(finals) or any(each >= r for each in late):
                if r < len(s_list) and s_list[r] is not None:
                    k, g = s_list[r]
                    square_bank(k, g)
                    squared(k, r)
                elif r < len(s_list) or r % 2 == HELP_PHASE:
                    i = next_final(True)
                    if i is not None:
                        final_bank(i, True, False, r)
                item = v_list[at] if at < len(v_list) else "final"
                if item == "final":
                    i = next_final(False)
                    if i is not None:
                        final_bank(i, False, i >= len(finals) - ALONE, r)
                        at += 1
                else:
                    at += 1
                    if item is not None:
                        square_bank(item[0], item[1])
                        squared(item[0], r)
                for step, u in plan.get(r, []):
                    step(u)
                    if step == keep_rb:
                        ready += sum(1 for each in finals if each[0] == u)
                for view, tile in late.get(r, []):
                    nc.sync.dma_start(out=view, in_=tile)
                ahead = max(item[0] for item in s_list[0:r + AHEAD] if item is not None)
                if r == 4 or (r > 4 and ahead // 4 >= prepared and prepared < 2 * B):
                    quantise_x(prepared // 2, prepared % 2)
                    prepared += 1
                    if prepared < 2 * B:
                        regroup_x(prepared // 2, prepared % 2)
                r += 1
